import numpy as np
import ml_dtypes


def mxq(x, axis, fmt="e4m3"):
    dtype, down = {"e4m3": (ml_dtypes.float8_e4m3fn, 7), "e5m2": (ml_dtypes.float8_e5m2, 14)}[fmt]
    v = np.moveaxis(np.asarray(x, np.float32).astype(ml_dtypes.bfloat16).astype(np.float64), axis, -1)
    blocks = v.reshape(v.shape[:-1] + (-1, 32))
    amax = np.abs(blocks).max(-1, keepdims=True)
    byte = np.maximum(np.where(amax > 0, np.frexp(amax)[1] - 1 + 127, 0) - down, 1)
    scale = np.exp2(byte - 127.0)
    codes = (blocks / scale).astype(np.float32).astype(dtype).astype(np.float64)
    return np.moveaxis((codes * scale).reshape(v.shape), -1, axis)


WIDE = False


def mx_kscale(k):
    if not WIDE:
        return np.ones(k)
    levels = np.array([10, -10, 5, -5, 0])
    a = np.random.permutation(np.resize(levels, k // 512 * 4)).reshape(k // 512, 4)
    idx = np.arange(k)
    return np.exp2(a[idx // 512, idx % 128 // 32])


BF16 = ml_dtypes.bfloat16


def bf(x):
    return np.asarray(x, np.float32).astype(BF16)


def f64(x):
    return np.asarray(x).astype(np.float64)


E2M1 = np.array([0.0, 0.5, 1.0, 1.5, 2.0, 3.0, 4.0, 6.0, -0.0, -0.5, -1.0, -1.5, -2.0, -3.0, -4.0, -6.0])


def pack_weight(w, fmt):
    k, n = w.shape
    w = f64(bf(w)).reshape(k // 32, 32, n)
    amax = np.abs(w).max(1)
    if fmt == "e4m3":
        byte = np.frexp(amax)[1] - 1 + 127 - 7
    else:
        mant, ex = np.frexp(amax / 6.0)
        byte = np.where(mant > 0.5, ex, ex - 1) + 127
    byte = np.clip(np.where(amax > 0, byte, 1), 1, 254)
    scaled = (w * np.exp2(127.0 - byte)[:, None, :]).reshape(k, n).astype(np.float32)
    by_word = np.ascontiguousarray(scaled.reshape(k // 512, 128, 4, n).transpose(0, 1, 3, 2))
    if fmt == "e4m3":
        words = by_word.astype(ml_dtypes.float8_e4m3fn).view(np.uint8)
    else:
        c = by_word.astype(ml_dtypes.float4_e2m1fn).view(np.uint8) & 0xF
        words = c[..., 0::2] | (c[..., 1::2] << 4)
    return np.ascontiguousarray(words), np.ascontiguousarray(byte.astype(np.uint8).reshape(k // 512, 16, n))


def unpack_weight(words, scales, fmt):
    g, p, n, _ = words.shape
    if fmt == "e4m3":
        vals = np.ascontiguousarray(words).view(ml_dtypes.float8_e4m3fn).astype(np.float64)
    else:
        nib = np.empty((g, p, n, 4), np.uint8)
        nib[..., 0::2] = words & 0xF
        nib[..., 1::2] = words >> 4
        vals = E2M1[nib]
    vals = vals * np.repeat(np.exp2(scales.astype(np.float64) - 127.0), 8, axis=1)[..., None]
    return vals.transpose(0, 1, 3, 2).reshape(g * 512, n)


B, L, C, KS, NL, BH, R = 1, 128, 512, 4, 24, 64, 4
OUT = 2 * BH * NL
FMT = "e4m3"


def setup_inputs():
    s, t = mx_kscale(C), mx_kscale(C)
    local_features = bf(np.random.standard_normal((B, L, C)) * s)
    wt = bf(np.random.standard_normal((C, C, KS)) / np.sqrt(C) / s[:, None, None] * t[None, :, None])
    bt = bf(np.random.standard_normal(C) * 0.5 * t)
    w1 = np.random.standard_normal((OUT, C)) / np.sqrt(C) / t[None, :]
    w1_words, w1_scales = pack_weight(np.ascontiguousarray(w1.T), FMT)
    b1 = bf(np.random.standard_normal(OUT) * 0.5)
    return {"local_features": local_features,
            "wt": wt,
            "bt": bt,
            "w1_words": w1_words,
            "w1_scales": w1_scales,
            "b1": b1}


def reference(local_features, wt, bt, w1_words, w1_scales, b1):
    xq = mxq(f64(local_features), 2, "e4m3")
    wq = mxq(f64(wt), 0, "e4m3")
    up = xq @ wq.reshape(C, C * KS)
    up = up.reshape(B, L, C, KS).transpose(0, 2, 1, 3).reshape(B, C, L * KS) + f64(bt)[None, :, None]
    y = (unpack_weight(w1_words, w1_scales, FMT).T @ mxq(up, 1, "e4m3")) + f64(b1)[None, :, None]
    y = np.tile(y, (1, 1, R))
    y = y.reshape(B, NL, 2 * BH, L * KS * R)
    return np.ascontiguousarray(y.transpose(2, 0, 1, 3))

@@ -1,0 +1,169 @@
+from contextlib import ExitStack
+
+import concourse.mybir as mybir
+from concourse.masks import make_identity
+
+F32 = mybir.dt.float32
+BF16 = mybir.dt.bfloat16
+I32 = mybir.dt.int32
+U32 = mybir.dt.uint32
+U8 = mybir.dt.uint8
+FP8X4 = mybir.dt.float8_e4m3fn_x4
+ADD = mybir.AluOpType.add
+IDENTITY = mybir.ActivationFunctionType.Identity
+
+P = 128
+PACK = 4
+L = 128
+C = 512
+KS = 4
+T = L * KS
+R = 4
+OUT = 3072
+N_BLOCKS = OUT // P
+HALVES = 2
+Q_HALF = P // HALVES
+W1_CHUNKS = 3
+Y_BUFS = 6
+ACC_BANKS = 6
+
+FLOPS = 2 * L * C * C * KS + 2 * OUT * C * T
+
+
+def tile_conditionalfeaturesupsample_kernel(
+    tc, local_features, wt, bt, w1_words, w1_scales, b1, out
+):
+    nc = tc.nc
+    with ExitStack() as ctx:
+        keep = ctx.enter_context(tc.tile_pool(name="keep", bufs=1))
+        y_pool = ctx.enter_context(tc.tile_pool(name="y_pool", bufs=Y_BUFS))
+        setup_psum = ctx.enter_context(tc.psum_pool(name="setup_psum", bufs=1))
+        acc_psum = ctx.enter_context(tc.psum_pool(name="acc_psum", bufs=ACC_BANKS))
+
+        ident = keep.tile([P, P], F32)
+        make_identity(nc, ident[:])
+        w1_planes = keep.tile([P, OUT], U8, align_bytes=64)
+        nc.vector.memset(w1_planes[:].bitcast(I32), 0)
+        b1_rows = keep.tile([P, P], BF16)
+        nc.gpsimd.memset(b1_rows[:], 0.0)
+
+        x_sb = keep.tile([P, C], BF16)
+        nc.sync.dma_start(out=x_sb[:], in_=local_features[0])
+        wt_raw = keep.tile([P, PACK, C * KS], BF16)
+        wt_rows = wt.rearrange("(p c) o k -> p c (o k)", c=PACK)
+        half_cols = C * KS // HALVES
+        for h in range(HALVES):
+            cols = slice(h * half_cols, (h + 1) * half_cols)
+            nc.sync.dma_start(out=wt_raw[:, :, cols], in_=wt_rows[:, :, cols])
+        for r in range(4):
+            nc.sync.dma_start(
+                out=w1_planes[r:P:32, :].bitcast(I32), in_=w1_scales[0, r:16:4, :].bitcast(I32)
+            )
+        w1_sb = keep.tile([P, OUT], U32, align_bytes=64)
+        w1_dram = w1_words[0].rearrange("p n t -> p (n t)").bitcast(I32)
+        chunk = OUT // W1_CHUNKS
+        for i in range(W1_CHUNKS):
+            cols = slice(i * chunk, (i + 1) * chunk)
+            nc.sync.dma_start(out=w1_sb[:, cols].bitcast(I32), in_=w1_dram[:, cols])
+        bt_bf = keep.tile([P, PACK], BF16)
+        nc.scalar.dma_start(out=bt_bf[:], in_=bt.rearrange("(q j) -> q j", j=PACK))
+        nc.scalar.dma_start(out=b1_rows[0:N_BLOCKS, :], in_=b1.rearrange("(n p) -> n p", p=P))
+
+        x_words_f32 = x_sb[:].bitcast(F32)
+        xt = setup_psum.tile([P, 2, L], F32)
+        for u in range(2):
+            nc.tensor.transpose(xt[:, u, :], x_words_f32[:, u : C // 2 : 2], ident[:])
+        x_grouped = keep.tile([P, L * PACK], BF16, align_bytes=64)
+        nc.vector.tensor_copy(
+            out=x_grouped[:].bitcast(F32).rearrange("p (l u) -> p l u", u=2),
+            in_=xt[:].rearrange("p u l -> p l u"),
+        )
+        x_codes = keep.tile([P, L], U32, align_bytes=64)
+        x_scales = keep.tile([P, L], U8, align_bytes=64)
+        nc.vector.quantize_mx(out=x_codes[:].bitcast(FP8X4), scales=x_scales[:], in_=x_grouped[:])
+
+        bt_f32 = keep.tile([P, PACK], F32)
+        nc.vector.tensor_copy(out=bt_f32[:], in_=bt_bf[:])
+        b1_rows_f32 = keep.tile([P, P], F32)
+        nc.vector.tensor_copy(out=b1_rows_f32[:], in_=b1_rows[:])
+        b1_t = setup_psum.tile([P, P], F32)
+        nc.tensor.transpose(b1_t[:], b1_rows_f32[:], ident[:])
+        b1_sb = keep.tile([P, N_BLOCKS], F32)
+        nc.vector.tensor_copy(out=b1_sb[:], in_=b1_t[:, 0:N_BLOCKS])
+
+        wt_grouped = keep.tile([P, KS, PACK, P, PACK], BF16, align_bytes=64)
+        wt_codes = keep.tile([P, KS, PACK, P], U32, align_bytes=64)
+        wt_scales = keep.tile([P, KS, PACK, P], U8, align_bytes=64)
+        wt_raw5 = wt_raw[:].rearrange("p c (q j k) -> p c q j k", j=PACK, k=KS)
+        for h in range(HALVES):
+            qs = slice(h * Q_HALF, (h + 1) * Q_HALF)
+            for j in range(PACK):
+                dst = wt_grouped[:, :, j, qs, :].rearrange("p k q c -> p q c k")
+                src = wt_raw5[:, :, qs, j, :].rearrange("p c q k -> p q c k")
+                if j < PACK // 2:
+                    nc.vector.tensor_copy(out=dst, in_=src)
+                else:
+                    nc.scalar.copy(out=dst, in_=src)
+            for j in range(PACK):
+                for k in range(KS):
+                    nc.vector.quantize_mx(
+                        out=wt_codes[:, k, j, qs].bitcast(FP8X4),
+                        scales=wt_scales[:, k, j, qs],
+                        in_=wt_grouped[:, k, j, qs, :].rearrange("p q c -> p (q c)"),
+                    )
+
+        up_grouped = keep.tile([P, KS, L, PACK], BF16, align_bytes=64)
+        up_codes = keep.tile([P, KS, L], U32, align_bytes=64)
+        up_scales = keep.tile([P, KS, L], U8, align_bytes=64)
+        for k in range(KS):
+            up_acc = acc_psum.tile([P, PACK, L], F32, tag="acc")
+            for j in range(PACK):
+                nc.tensor.matmul_mx(
+                    out=up_acc[:, j, :],
+                    lhsT=wt_codes[:, k, j, :].bitcast(FP8X4),
+                    lhsT_scale=wt_scales[:, k, j, :],
+                    rhs=x_codes[:].bitcast(FP8X4),
+                    rhs_scale=x_scales[:],
+                    start=True,
+                    stop=True,
+                )
+            nc.vector.tensor_tensor(
+                out=up_grouped[:, k],
+                in0=up_acc[:].rearrange("q j l -> q l j"),
+                in1=bt_f32[:].unsqueeze(1).to_broadcast([P, L, PACK]),
+                op=ADD,
+            )
+            nc.vector.quantize_mx(
+                out=up_codes[:, k, :].bitcast(FP8X4),
+                scales=up_scales[:, k, :],
+                in_=up_grouped[:, k].rearrange("q l j -> q (l j)"),
+            )
+
+        for pair in range(N_BLOCKS // 2):
+            y_sb = y_pool.tile([P, 2, R, L, KS], F32)
+            for e in range(2):
+                n = 2 * pair + e
+                n_cols = slice(n * P, (n + 1) * P)
+                y_acc = acc_psum.tile([P, KS, L], F32, tag="acc")
+                nc.tensor.matmul_mx(
+                    out=y_acc[:].rearrange("p k l -> p (k l)"),
+                    lhsT=w1_sb[:, n_cols].bitcast(FP8X4),
+                    lhsT_scale=w1_planes[:, n_cols],
+                    rhs=up_codes[:].rearrange("q k l -> q (k l)").bitcast(FP8X4),
+                    rhs_scale=up_scales[:].rearrange("q k l -> q (k l)"),
+                    start=True,
+                    stop=True,
+                )
+                repeated = y_acc[:].rearrange("p k l -> p l k").unsqueeze(1).to_broadcast([P, R, L, KS])
+                if e == 0:
+                    nc.vector.tensor_scalar(
+                        out=y_sb[:, e], in0=repeated, scalar1=b1_sb[:, n : n + 1], scalar2=None, op0=ADD
+                    )
+                else:
+                    nc.scalar.activation(
+                        out=y_sb[:, e], in_=repeated, func=IDENTITY, bias=b1_sb[:, n : n + 1]
+                    )
+            nc.sync.dma_start(
+                out=out[:, 0, 2 * pair : 2 * pair + 2, :],
+                in_=y_sb[:].rearrange("p e r l k -> p e (r l k)"),
+            )

@@ -25,9 +25,17 @@ HALVES = 2
 Q_HALF = P // HALVES
 W1_CHUNKS = 3
 Y_BUFS = 6
+FIRST_PAIRS = 1
 ACC_BANKS = 6
 
 FLOPS = 2 * L * C * C * KS + 2 * OUT * C * T
+
+
+def add_bias_out_of_psum(nc, on_vector, dst, src, bias):
+    if on_vector:
+        nc.vector.tensor_scalar(out=dst, in0=src, scalar1=bias, scalar2=None, op0=ADD)
+    else:
+        nc.scalar.activation(out=dst, in_=src, func=IDENTITY, bias=bias)
 
 
 def tile_conditionalfeaturesupsample_kernel(
@@ -39,14 +47,20 @@ def tile_conditionalfeaturesupsample_kernel(
         y_pool = ctx.enter_context(tc.tile_pool(name="y_pool", bufs=Y_BUFS))
         setup_psum = ctx.enter_context(tc.psum_pool(name="setup_psum", bufs=1))
         acc_psum = ctx.enter_context(tc.psum_pool(name="acc_psum", bufs=ACC_BANKS))
+        ctx.enter_context(tc.manual_schedule())
 
-        ident = keep.tile([P, P], F32)
-        make_identity(nc, ident[:])
-        w1_planes = keep.tile([P, OUT], U8, align_bytes=64)
-        nc.vector.memset(w1_planes[:].bitcast(I32), 0)
         b1_rows = keep.tile([P, P], BF16)
         nc.gpsimd.memset(b1_rows[:], 0.0)
+        ident_f32 = keep.tile([P, P], F32)
+        make_identity(nc, ident_f32[:])
+        ident_bf = keep.tile([P, P], BF16)
+        make_identity(nc, ident_bf[:])
+        w1_planes = keep.tile([P, OUT], U8, align_bytes=64)
+        nc.vector.memset(w1_planes[:].bitcast(I32), 0)
 
+        bt_sb = keep.tile([P, PACK], BF16)
+        nc.scalar.dma_start(out=bt_sb[:], in_=bt.rearrange("(q j) -> q j", j=PACK))
+        nc.scalar.dma_start(out=b1_rows[0:N_BLOCKS, :], in_=b1.rearrange("(n p) -> n p", p=P))
         x_sb = keep.tile([P, C], BF16)
         nc.sync.dma_start(out=x_sb[:], in_=local_features[0])
         wt_raw = keep.tile([P, PACK, C * KS], BF16)
@@ -65,37 +79,30 @@ def tile_conditionalfeaturesupsample_kernel(
         for i in range(W1_CHUNKS):
             cols = slice(i * chunk, (i + 1) * chunk)
             nc.sync.dma_start(out=w1_sb[:, cols].bitcast(I32), in_=w1_dram[:, cols])
-        bt_bf = keep.tile([P, PACK], BF16)
-        nc.scalar.dma_start(out=bt_bf[:], in_=bt.rearrange("(q j) -> q j", j=PACK))
-        nc.scalar.dma_start(out=b1_rows[0:N_BLOCKS, :], in_=b1.rearrange("(n p) -> n p", p=P))
 
         x_words_f32 = x_sb[:].bitcast(F32)
         xt = setup_psum.tile([P, 2, L], F32)
         for u in range(2):
-            nc.tensor.transpose(xt[:, u, :], x_words_f32[:, u : C // 2 : 2], ident[:])
+            nc.tensor.transpose(xt[:, u, :], x_words_f32[:, u : C // 2 : 2], ident_f32[:])
         x_grouped = keep.tile([P, L * PACK], BF16, align_bytes=64)
         nc.vector.tensor_copy(
             out=x_grouped[:].bitcast(F32).rearrange("p (l u) -> p l u", u=2),
             in_=xt[:].rearrange("p u l -> p l u"),
         )
+        b1_t = setup_psum.tile([P, P], BF16)
+        nc.tensor.transpose(b1_t[:], b1_rows[:], ident_bf[:])
+        b1_sb = keep.tile([P, N_BLOCKS], F32)
+        nc.scalar.copy(out=b1_sb[:], in_=b1_t[:, 0:N_BLOCKS])
         x_codes = keep.tile([P, L], U32, align_bytes=64)
         x_scales = keep.tile([P, L], U8, align_bytes=64)
         nc.vector.quantize_mx(out=x_codes[:].bitcast(FP8X4), scales=x_scales[:], in_=x_grouped[:])
-
-        bt_f32 = keep.tile([P, PACK], F32)
-        nc.vector.tensor_copy(out=bt_f32[:], in_=bt_bf[:])
-        b1_rows_f32 = keep.tile([P, P], F32)
-        nc.vector.tensor_copy(out=b1_rows_f32[:], in_=b1_rows[:])
-        b1_t = setup_psum.tile([P, P], F32)
-        nc.tensor.transpose(b1_t[:], b1_rows_f32[:], ident[:])
-        b1_sb = keep.tile([P, N_BLOCKS], F32)
-        nc.vector.tensor_copy(out=b1_sb[:], in_=b1_t[:, 0:N_BLOCKS])
 
         wt_grouped = keep.tile([P, KS, PACK, P, PACK], BF16, align_bytes=64)
         wt_codes = keep.tile([P, KS, PACK, P], U32, align_bytes=64)
         wt_scales = keep.tile([P, KS, PACK, P], U8, align_bytes=64)
         wt_raw5 = wt_raw[:].rearrange("p c (q j k) -> p c q j k", j=PACK, k=KS)
-        for h in range(HALVES):
+
+        def sort_half(h):
             qs = slice(h * Q_HALF, (h + 1) * Q_HALF)
             for j in range(PACK):
                 dst = wt_grouped[:, :, j, qs, :].rearrange("p k q c -> p q c k")
@@ -104,13 +111,22 @@ def tile_conditionalfeaturesupsample_kernel(
                     nc.vector.tensor_copy(out=dst, in_=src)
                 else:
                     nc.scalar.copy(out=dst, in_=src)
-            for j in range(PACK):
+
+        def quantise_half(h, js):
+            qs = slice(h * Q_HALF, (h + 1) * Q_HALF)
+            for j in js:
                 for k in range(KS):
                     nc.vector.quantize_mx(
                         out=wt_codes[:, k, j, qs].bitcast(FP8X4),
                         scales=wt_scales[:, k, j, qs],
                         in_=wt_grouped[:, k, j, qs, :].rearrange("p q c -> p (q c)"),
                     )
+
+        sort_half(0)
+        quantise_half(0, (0, 1))
+        sort_half(1)
+        quantise_half(0, (2, 3))
+        quantise_half(1, (0, 1, 2, 3))
 
         up_grouped = keep.tile([P, KS, L, PACK], BF16, align_bytes=64)
         up_codes = keep.tile([P, KS, L], U32, align_bytes=64)
@@ -130,7 +146,7 @@ def tile_conditionalfeaturesupsample_kernel(
             nc.vector.tensor_tensor(
                 out=up_grouped[:, k],
                 in0=up_acc[:].rearrange("q j l -> q l j"),
-                in1=bt_f32[:].unsqueeze(1).to_broadcast([P, L, PACK]),
+                in1=bt_sb[:].unsqueeze(1).to_broadcast([P, L, PACK]),
                 op=ADD,
             )
             nc.vector.quantize_mx(
@@ -139,30 +155,39 @@ def tile_conditionalfeaturesupsample_kernel(
                 in_=up_grouped[:, k].rearrange("q l j -> q (l j)"),
             )
 
-        for pair in range(N_BLOCKS // 2):
-            y_sb = y_pool.tile([P, 2, R, L, KS], F32)
+        def second_product(n):
+            n_cols = slice(n * P, (n + 1) * P)
+            y_acc = acc_psum.tile([P, KS, L], F32, tag="acc")
+            nc.tensor.matmul_mx(
+                out=y_acc[:].rearrange("p k l -> p (k l)"),
+                lhsT=w1_sb[:, n_cols].bitcast(FP8X4),
+                lhsT_scale=w1_planes[:, n_cols],
+                rhs=up_codes[:].rearrange("q k l -> q (k l)").bitcast(FP8X4),
+                rhs_scale=up_scales[:].rearrange("q k l -> q (k l)"),
+                start=True,
+                stop=True,
+            )
+            return y_acc[:].rearrange("p k l -> p l k")
+
+        for pair in range(FIRST_PAIRS):
+            y_once = keep.tile([P, 2, L, KS], F32, name="y_once_%d" % pair)
+            banks = [second_product(2 * pair + e) for e in range(2)]
             for e in range(2):
                 n = 2 * pair + e
-                n_cols = slice(n * P, (n + 1) * P)
-                y_acc = acc_psum.tile([P, KS, L], F32, tag="acc")
-                nc.tensor.matmul_mx(
-                    out=y_acc[:].rearrange("p k l -> p (k l)"),
-                    lhsT=w1_sb[:, n_cols].bitcast(FP8X4),
-                    lhsT_scale=w1_planes[:, n_cols],
-                    rhs=up_codes[:].rearrange("q k l -> q (k l)").bitcast(FP8X4),
-                    rhs_scale=up_scales[:].rearrange("q k l -> q (k l)"),
-                    start=True,
-                    stop=True,
-                )
-                repeated = y_acc[:].rearrange("p k l -> p l k").unsqueeze(1).to_broadcast([P, R, L, KS])
-                if e == 0:
-                    nc.vector.tensor_scalar(
-                        out=y_sb[:, e], in0=repeated, scalar1=b1_sb[:, n : n + 1], scalar2=None, op0=ADD
+                add_bias_out_of_psum(nc, e == 0, y_once[:, e], banks[e], b1_sb[:, n : n + 1])
+            for e in range(2):
+                for r in range(R):
+                    nc.sync.dma_start(
+                        out=out[:, 0, 2 * pair + e, r * T : (r + 1) * T],
+                        in_=y_once[:, e].rearrange("p l k -> p (l k)"),
                     )
-                else:
-                    nc.scalar.activation(
-                        out=y_sb[:, e], in_=repeated, func=IDENTITY, bias=b1_sb[:, n : n + 1]
-                    )
+        for pair in range(FIRST_PAIRS, N_BLOCKS // 2):
+            y_sb = y_pool.tile([P, 2, R, L, KS], F32)
+            banks = [second_product(2 * pair + e) for e in range(2)]
+            for e in range(2):
+                n = 2 * pair + e
+                repeated = banks[e].unsqueeze(1).to_broadcast([P, R, L, KS])
+                add_bias_out_of_psum(nc, e == 0, y_sb[:, e], repeated, b1_sb[:, n : n + 1])
             nc.sync.dma_start(
                 out=out[:, 0, 2 * pair : 2 * pair + 2, :],
                 in_=y_sb[:].rearrange("p e r l k -> p e (r l k)"),

@@ -21,8 +21,9 @@ T = L * KS
 R = 4
 OUT = 3072
 N_BLOCKS = OUT // P
-HALVES = 2
-Q_HALF = P // HALVES
+WT_CHUNKS = 4
+Q_CHUNK = P // WT_CHUNKS
+Q_HALF = 64
 W1_CHUNKS = 3
 Y_BUFS = 6
 FIRST_PAIRS = 1
@@ -55,6 +56,7 @@ def tile_conditionalfeaturesupsample_kernel(
         make_identity(nc, ident_f32[:])
         ident_bf = keep.tile([P, P], BF16)
         make_identity(nc, ident_bf[:])
+        bt_f32 = keep.tile([P, PACK], F32)
         w1_planes = keep.tile([P, OUT], U8, align_bytes=64)
         nc.vector.memset(w1_planes[:].bitcast(I32), 0)
 
@@ -65,9 +67,9 @@ def tile_conditionalfeaturesupsample_kernel(
         nc.sync.dma_start(out=x_sb[:], in_=local_features[0])
         wt_raw = keep.tile([P, PACK, C * KS], BF16)
         wt_rows = wt.rearrange("(p c) o k -> p c (o k)", c=PACK)
-        half_cols = C * KS // HALVES
-        for h in range(HALVES):
-            cols = slice(h * half_cols, (h + 1) * half_cols)
+        chunk_cols = C * KS // WT_CHUNKS
+        for a in range(WT_CHUNKS):
+            cols = slice(a * chunk_cols, (a + 1) * chunk_cols)
             nc.sync.dma_start(out=wt_raw[:, :, cols], in_=wt_rows[:, :, cols])
         for r in range(4):
             nc.sync.dma_start(
@@ -80,6 +82,7 @@ def tile_conditionalfeaturesupsample_kernel(
             cols = slice(i * chunk, (i + 1) * chunk)
             nc.sync.dma_start(out=w1_sb[:, cols].bitcast(I32), in_=w1_dram[:, cols])
 
+        nc.gpsimd.tensor_copy(out=bt_f32[:], in_=bt_sb[:])
         x_words_f32 = x_sb[:].bitcast(F32)
         xt = setup_psum.tile([P, 2, L], F32)
         for u in range(2):
@@ -102,8 +105,8 @@ def tile_conditionalfeaturesupsample_kernel(
         wt_scales = keep.tile([P, KS, PACK, P], U8, align_bytes=64)
         wt_raw5 = wt_raw[:].rearrange("p c (q j k) -> p c q j k", j=PACK, k=KS)
 
-        def sort_half(h):
-            qs = slice(h * Q_HALF, (h + 1) * Q_HALF)
+        def sort_chunk(a):
+            qs = slice(a * Q_CHUNK, (a + 1) * Q_CHUNK)
             for j in range(PACK):
                 dst = wt_grouped[:, :, j, qs, :].rearrange("p k q c -> p q c k")
                 src = wt_raw5[:, :, qs, j, :].rearrange("p c q k -> p q c k")
@@ -112,30 +115,21 @@ def tile_conditionalfeaturesupsample_kernel(
                 else:
                     nc.scalar.copy(out=dst, in_=src)
 
-        def quantise_half(h, js):
+        def quantise_half(h, j):
             qs = slice(h * Q_HALF, (h + 1) * Q_HALF)
-            for j in js:
-                for k in range(KS):
-                    nc.vector.quantize_mx(
-                        out=wt_codes[:, k, j, qs].bitcast(FP8X4),
-                        scales=wt_scales[:, k, j, qs],
-                        in_=wt_grouped[:, k, j, qs, :].rearrange("p q c -> p (q c)"),
-                    )
+            for k in range(KS):
+                nc.vector.quantize_mx(
+                    out=wt_codes[:, k, j, qs].bitcast(FP8X4),
+                    scales=wt_scales[:, k, j, qs],
+                    in_=wt_grouped[:, k, j, qs, :].rearrange("p q c -> p (q c)"),
+                )
 
-        sort_half(0)
-        quantise_half(0, (0, 1))
-        sort_half(1)
-        quantise_half(0, (2, 3))
-        quantise_half(1, (0, 1, 2, 3))
+        up_acc = [acc_psum.tile([P, PACK, L], F32, tag="acc", name="up_acc_%d" % k) for k in range(KS)]
 
-        up_grouped = keep.tile([P, KS, L, PACK], BF16, align_bytes=64)
-        up_codes = keep.tile([P, KS, L], U32, align_bytes=64)
-        up_scales = keep.tile([P, KS, L], U8, align_bytes=64)
-        for k in range(KS):
-            up_acc = acc_psum.tile([P, PACK, L], F32, tag="acc")
-            for j in range(PACK):
+        def first_product(j):
+            for k in range(KS):
                 nc.tensor.matmul_mx(
-                    out=up_acc[:, j, :],
+                    out=up_acc[k][:, j, :],
                     lhsT=wt_codes[:, k, j, :].bitcast(FP8X4),
                     lhsT_scale=wt_scales[:, k, j, :],
                     rhs=x_codes[:].bitcast(FP8X4),
@@ -143,17 +137,45 @@ def tile_conditionalfeaturesupsample_kernel(
                     start=True,
                     stop=True,
                 )
-            nc.vector.tensor_tensor(
-                out=up_grouped[:, k],
-                in0=up_acc[:].rearrange("q j l -> q l j"),
-                in1=bt_sb[:].unsqueeze(1).to_broadcast([P, L, PACK]),
-                op=ADD,
-            )
+
+        sort_chunk(0)
+        sort_chunk(1)
+        quantise_half(0, 0)
+        quantise_half(0, 1)
+        sort_chunk(2)
+        quantise_half(0, 2)
+        quantise_half(0, 3)
+        sort_chunk(3)
+        for j in range(PACK):
+            quantise_half(1, j)
+            first_product(j)
+
+        up_grouped = keep.tile([P, KS, L, PACK], BF16, align_bytes=64)
+        up_codes = keep.tile([P, KS, L], U32, align_bytes=64)
+        up_scales = keep.tile([P, KS, L], U8, align_bytes=64)
+
+        def quantise_up(k):
             nc.vector.quantize_mx(
                 out=up_codes[:, k, :].bitcast(FP8X4),
                 scales=up_scales[:, k, :],
                 in_=up_grouped[:, k].rearrange("q l j -> q (l j)"),
             )
+
+        for j in range(PACK):
+            nc.scalar.activation(
+                out=up_grouped[:, 0, :, j], in_=up_acc[0][:, j, :], func=IDENTITY, bias=bt_f32[:, j : j + 1]
+            )
+        for k in range(1, KS):
+            nc.vector.tensor_tensor(
+                out=up_grouped[:, k],
+                in0=up_acc[k][:].rearrange("q j l -> q l j"),
+                in1=bt_f32[:].unsqueeze(1).to_broadcast([P, L, PACK]),
+                op=ADD,
+            )
+            if k > 1:
+                quantise_up(k - 1)
+        quantise_up(0)
+        quantise_up(KS - 1)
 
         def second_product(n):
             n_cols = slice(n * P, (n + 1) * P)

@@ -28,6 +28,8 @@ W1_CHUNKS = 3
 Y_BUFS = 6
 FIRST_PAIRS = 1
 ACC_BANKS = 6
+HALVES = 2
+LH = L // HALVES
 
 FLOPS = 2 * L * C * C * KS + 2 * OUT * C * T
 
@@ -150,66 +152,98 @@ def tile_conditionalfeaturesupsample_kernel(
             quantise_half(1, j)
             first_product(j)
 
-        up_grouped = keep.tile([P, KS, L, PACK], BF16, align_bytes=64)
-        up_codes = keep.tile([P, KS, L], U32, align_bytes=64)
-        up_scales = keep.tile([P, KS, L], U8, align_bytes=64)
+        up_grouped = keep.tile([P, HALVES, KS, LH, PACK], BF16, align_bytes=64)
+        up_codes = keep.tile([P, HALVES, KS, LH], U32, align_bytes=64)
+        up_scales = keep.tile([P, HALVES, KS, LH], U8, align_bytes=64)
 
-        def quantise_up(k):
+        def quantise_up(h):
             nc.vector.quantize_mx(
-                out=up_codes[:, k, :].bitcast(FP8X4),
-                scales=up_scales[:, k, :],
-                in_=up_grouped[:, k].rearrange("q l j -> q (l j)"),
+                out=up_codes[:, h].rearrange("q k l -> q (k l)").bitcast(FP8X4),
+                scales=up_scales[:, h].rearrange("q k l -> q (k l)"),
+                in_=up_grouped[:, h].rearrange("q k l j -> q (k l j)"),
             )
 
-        for j in range(PACK):
-            nc.scalar.activation(
-                out=up_grouped[:, 0, :, j], in_=up_acc[0][:, j, :], func=IDENTITY, bias=bt_f32[:, j : j + 1]
-            )
-        for k in range(1, KS):
+        def up_on_scalar(h):
+            for j in range(PACK):
+                nc.scalar.activation(
+                    out=up_grouped[:, h, 0, :, j],
+                    in_=up_acc[0][:, j, h * LH : (h + 1) * LH],
+                    func=IDENTITY,
+                    bias=bt_f32[:, j : j + 1],
+                )
+
+        def up_on_vector(h, k):
             nc.vector.tensor_tensor(
-                out=up_grouped[:, k],
-                in0=up_acc[k][:].rearrange("q j l -> q l j"),
-                in1=bt_f32[:].unsqueeze(1).to_broadcast([P, L, PACK]),
+                out=up_grouped[:, h, k],
+                in0=up_acc[k][:, :, h * LH : (h + 1) * LH].rearrange("q j l -> q l j"),
+                in1=bt_f32[:].unsqueeze(1).to_broadcast([P, LH, PACK]),
                 op=ADD,
             )
-            if k > 1:
-                quantise_up(k - 1)
-        quantise_up(0)
-        quantise_up(KS - 1)
 
-        def second_product(n):
+        def second_product_half(n, h):
             n_cols = slice(n * P, (n + 1) * P)
-            y_acc = acc_psum.tile([P, KS, L], F32, tag="acc")
+            y_acc = acc_psum.tile([P, KS, LH], F32, tag="acc", name="y_half_%d_%d" % (n, h))
             nc.tensor.matmul_mx(
                 out=y_acc[:].rearrange("p k l -> p (k l)"),
                 lhsT=w1_sb[:, n_cols].bitcast(FP8X4),
                 lhsT_scale=w1_planes[:, n_cols],
-                rhs=up_codes[:].rearrange("q k l -> q (k l)").bitcast(FP8X4),
-                rhs_scale=up_scales[:].rearrange("q k l -> q (k l)"),
+                rhs=up_codes[:, h].rearrange("q k l -> q (k l)").bitcast(FP8X4),
+                rhs_scale=up_scales[:, h].rearrange("q k l -> q (k l)"),
                 start=True,
                 stop=True,
             )
             return y_acc[:].rearrange("p k l -> p l k")
 
-        for pair in range(FIRST_PAIRS):
-            y_once = keep.tile([P, 2, L, KS], F32, name="y_once_%d" % pair)
-            banks = [second_product(2 * pair + e) for e in range(2)]
+        def second_product(n):
+            n_cols = slice(n * P, (n + 1) * P)
+            y_acc = acc_psum.tile([P, HALVES, KS, LH], F32, tag="acc")
+            nc.tensor.matmul_mx(
+                out=y_acc[:].rearrange("p h k l -> p (h k l)"),
+                lhsT=w1_sb[:, n_cols].bitcast(FP8X4),
+                lhsT_scale=w1_planes[:, n_cols],
+                rhs=up_codes[:].rearrange("q h k l -> q (h k l)").bitcast(FP8X4),
+                rhs_scale=up_scales[:].rearrange("q h k l -> q (h k l)"),
+                start=True,
+                stop=True,
+            )
+            return [y_acc[:, h].rearrange("p k l -> p l k") for h in range(HALVES)]
+
+        y_once = keep.tile([P, 2, L, KS], F32)
+
+        def first_pair_out(h, banks):
+            ls = slice(h * LH, (h + 1) * LH)
             for e in range(2):
-                n = 2 * pair + e
-                add_bias_out_of_psum(nc, e == 0, y_once[:, e], banks[e], b1_sb[:, n : n + 1])
-            for e in range(2):
-                for r in range(R):
-                    nc.sync.dma_start(
-                        out=out[:, 0, 2 * pair + e, r * T : (r + 1) * T],
-                        in_=y_once[:, e].rearrange("p l k -> p (l k)"),
-                    )
-        for pair in range(FIRST_PAIRS, N_BLOCKS // 2):
+                add_bias_out_of_psum(nc, e == 0, y_once[:, e, ls], banks[e], b1_sb[:, e : e + 1])
+            for r in range(R):
+                nc.sync.dma_start(
+                    out=out[:, 0, 0:2, r * T + h * LH * KS : r * T + (h + 1) * LH * KS],
+                    in_=y_once[:, :, ls].rearrange("p e l k -> p e (l k)"),
+                )
+
+        up_on_scalar(0)
+        for k in range(1, KS):
+            up_on_vector(0, k)
+        up_on_vector(1, 1)
+        quantise_up(0)
+        up_on_scalar(1)
+        banks_0 = [second_product_half(e, 0) for e in range(2)]
+        up_on_vector(1, 2)
+        up_on_vector(1, 3)
+        first_pair_out(0, banks_0)
+        quantise_up(1)
+        banks_1 = [second_product_half(e, 1) for e in range(2)]
+        first_pair_out(1, banks_1)
+
+        for pair in range(1, N_BLOCKS // 2):
             y_sb = y_pool.tile([P, 2, R, L, KS], F32)
             banks = [second_product(2 * pair + e) for e in range(2)]
-            for e in range(2):
-                n = 2 * pair + e
-                repeated = banks[e].unsqueeze(1).to_broadcast([P, R, L, KS])
-                add_bias_out_of_psum(nc, e == 0, y_sb[:, e], repeated, b1_sb[:, n : n + 1])
+            for h in range(HALVES):
+                for e in range(2):
+                    n = 2 * pair + e
+                    repeated = banks[e][h].unsqueeze(1).to_broadcast([P, R, LH, KS])
+                    add_bias_out_of_psum(
+                        nc, e == 0, y_sb[:, e, :, h * LH : (h + 1) * LH], repeated, b1_sb[:, n : n + 1]
+                    )
             nc.sync.dma_start(
                 out=out[:, 0, 2 * pair : 2 * pair + 2, :],
                 in_=y_sb[:].rearrange("p e r l k -> p e (r l k)"),

@@ -25,7 +25,8 @@ WT_CHUNKS = 4
 Q_CHUNK = P // WT_CHUNKS
 Q_HALF = 64
 W1_CHUNKS = 3
-Y_BUFS = 6
+Y_BUFS = 4
+GROUP = 4
 FIRST_PAIRS = 1
 ACC_BANKS = 6
 HALVES = 2
@@ -208,16 +209,31 @@ def tile_conditionalfeaturesupsample_kernel(
             )
             return [y_acc[:, h].rearrange("p k l -> p l k") for h in range(HALVES)]
 
-        y_once = keep.tile([P, 2, L, KS], F32)
+        def repeat_out_of_psum(on_vector, dst, bank_view, h, n):
+            add_bias_out_of_psum(
+                nc,
+                on_vector,
+                dst[:, :, h * LH : (h + 1) * LH],
+                bank_view.unsqueeze(1).to_broadcast([P, R, LH, KS]),
+                b1_sb[:, n : n + 1],
+            )
 
-        def first_pair_out(h, banks):
+        def block_out(on_vector, dst, n):
+            banks = second_product(n)
+            for h in range(HALVES):
+                repeat_out_of_psum(on_vector, dst, banks[h], h, n)
+
+        y_0 = keep.tile([P, L, KS], F32)
+        y_1 = keep.tile([P, R, L, KS], F32)
+        y_23 = keep.tile([P, 2, R, L, KS], F32)
+
+        def block_0_out(on_vector, h, bank_view):
             ls = slice(h * LH, (h + 1) * LH)
-            for e in range(2):
-                add_bias_out_of_psum(nc, e == 0, y_once[:, e, ls], banks[e], b1_sb[:, e : e + 1])
+            add_bias_out_of_psum(nc, on_vector, y_0[:, ls], bank_view, b1_sb[:, 0:1])
             for r in range(R):
                 nc.sync.dma_start(
-                    out=out[:, 0, 0:2, r * T + h * LH * KS : r * T + (h + 1) * LH * KS],
-                    in_=y_once[:, :, ls].rearrange("p e l k -> p e (l k)"),
+                    out=out[:, 0, 0, r * T + h * LH * KS : r * T + (h + 1) * LH * KS],
+                    in_=y_0[:, ls].rearrange("p l k -> p (l k)"),
                 )
 
         up_on_scalar(0)
@@ -226,25 +242,25 @@ def tile_conditionalfeaturesupsample_kernel(
         up_on_vector(1, 1)
         quantise_up(0)
         up_on_scalar(1)
-        banks_0 = [second_product_half(e, 0) for e in range(2)]
+        banks_0 = [second_product_half(n, 0) for n in range(2)]
         up_on_vector(1, 2)
         up_on_vector(1, 3)
-        first_pair_out(0, banks_0)
+        block_0_out(False, 0, banks_0[0])
+        repeat_out_of_psum(False, y_1, banks_0[1], 0, 1)
         quantise_up(1)
-        banks_1 = [second_product_half(e, 1) for e in range(2)]
-        first_pair_out(1, banks_1)
+        banks_1 = [second_product_half(n, 1) for n in range(2)]
+        block_0_out(True, 1, banks_1[0])
+        repeat_out_of_psum(True, y_1, banks_1[1], 1, 1)
+        nc.sync.dma_start(out=out[:, 0, 1, :], in_=y_1[:].rearrange("p r l k -> p (r l k)"))
+        block_out(False, y_23[:, 0], 2)
+        block_out(True, y_23[:, 1], 3)
+        nc.sync.dma_start(out=out[:, 0, 2:4, :], in_=y_23[:].rearrange("p e r l k -> p e (r l k)"))
 
-        for pair in range(1, N_BLOCKS // 2):
-            y_sb = y_pool.tile([P, 2, R, L, KS], F32)
-            banks = [second_product(2 * pair + e) for e in range(2)]
-            for h in range(HALVES):
-                for e in range(2):
-                    n = 2 * pair + e
-                    repeated = banks[e][h].unsqueeze(1).to_broadcast([P, R, LH, KS])
-                    add_bias_out_of_psum(
-                        nc, e == 0, y_sb[:, e, :, h * LH : (h + 1) * LH], repeated, b1_sb[:, n : n + 1]
-                    )
+        for n0 in range(GROUP, N_BLOCKS, GROUP):
+            y_sb = y_pool.tile([P, GROUP, R, L, KS], F32)
+            for e in range(GROUP):
+                block_out(e % 2 == 1, y_sb[:, e], n0 + e)
             nc.sync.dma_start(
-                out=out[:, 0, 2 * pair : 2 * pair + 2, :],
+                out=out[:, 0, n0 : n0 + GROUP, :],
                 in_=y_sb[:].rearrange("p e r l k -> p e (r l k)"),
             )

@@ -29,6 +29,7 @@ Y_BUFS = 4
 GROUP = 4
 FIRST_PAIRS = 1
 ACC_BANKS = 6
+VECTOR_J = 3
 HALVES = 2
 LH = L // HALVES
 
@@ -95,10 +96,6 @@ def tile_conditionalfeaturesupsample_kernel(
             out=x_grouped[:].bitcast(F32).rearrange("p (l u) -> p l u", u=2),
             in_=xt[:].rearrange("p u l -> p l u"),
         )
-        b1_t = setup_psum.tile([P, P], BF16)
-        nc.tensor.transpose(b1_t[:], b1_rows[:], ident_bf[:])
-        b1_sb = keep.tile([P, N_BLOCKS], F32)
-        nc.scalar.copy(out=b1_sb[:], in_=b1_t[:, 0:N_BLOCKS])
         x_codes = keep.tile([P, L], U32, align_bytes=64)
         x_scales = keep.tile([P, L], U8, align_bytes=64)
         nc.vector.quantize_mx(out=x_codes[:].bitcast(FP8X4), scales=x_scales[:], in_=x_grouped[:])
@@ -113,24 +110,22 @@ def tile_conditionalfeaturesupsample_kernel(
             for j in range(PACK):
                 dst = wt_grouped[:, :, j, qs, :].rearrange("p k q c -> p q c k")
                 src = wt_raw5[:, :, qs, j, :].rearrange("p c q k -> p q c k")
-                if j < PACK // 2:
+                if j < VECTOR_J:
                     nc.vector.tensor_copy(out=dst, in_=src)
                 else:
                     nc.scalar.copy(out=dst, in_=src)
 
-        def quantise_half(h, j):
-            qs = slice(h * Q_HALF, (h + 1) * Q_HALF)
-            for k in range(KS):
-                nc.vector.quantize_mx(
-                    out=wt_codes[:, k, j, qs].bitcast(FP8X4),
-                    scales=wt_scales[:, k, j, qs],
-                    in_=wt_grouped[:, k, j, qs, :].rearrange("p q c -> p (q c)"),
-                )
+        def quantise_tap(k):
+            nc.vector.quantize_mx(
+                out=wt_codes[:, k].rearrange("p j q -> p (j q)").bitcast(FP8X4),
+                scales=wt_scales[:, k].rearrange("p j q -> p (j q)"),
+                in_=wt_grouped[:, k].rearrange("p j q c -> p (j q c)"),
+            )
 
         up_acc = [acc_psum.tile([P, PACK, L], F32, tag="acc", name="up_acc_%d" % k) for k in range(KS)]
 
-        def first_product(j):
-            for k in range(KS):
+        def first_product(k):
+            for j in range(PACK):
                 nc.tensor.matmul_mx(
                     out=up_acc[k][:, j, :],
                     lhsT=wt_codes[:, k, j, :].bitcast(FP8X4),
@@ -141,17 +136,15 @@ def tile_conditionalfeaturesupsample_kernel(
                     stop=True,
                 )
 
-        sort_chunk(0)
-        sort_chunk(1)
-        quantise_half(0, 0)
-        quantise_half(0, 1)
-        sort_chunk(2)
-        quantise_half(0, 2)
-        quantise_half(0, 3)
-        sort_chunk(3)
-        for j in range(PACK):
-            quantise_half(1, j)
-            first_product(j)
+        for a in range(WT_CHUNKS):
+            sort_chunk(a)
+        b1_t = setup_psum.tile([P, P], BF16)
+        nc.tensor.transpose(b1_t[:], b1_rows[:], ident_bf[:])
+        b1_sb = keep.tile([P, N_BLOCKS], F32)
+        nc.scalar.copy(out=b1_sb[:], in_=b1_t[:, 0:N_BLOCKS])
+        for k in range(KS):
+            quantise_tap(k)
+            first_product(k)
 
         up_grouped = keep.tile([P, HALVES, KS, LH, PACK], BF16, align_bytes=64)
         up_codes = keep.tile([P, HALVES, KS, LH], U32, align_bytes=64)

@@ -115,6 +115,15 @@ def tile_conditionalfeaturesupsample_kernel(
                 else:
                     nc.scalar.copy(out=dst, in_=src)
 
+        def sort_tap(a, k, on_vector):
+            qs = slice(a * Q_CHUNK, (a + 1) * Q_CHUNK)
+            dst = wt_grouped[:, k, :, qs, :].rearrange("p j q c -> p q c j")
+            src = wt_raw5[:, :, qs, :, k].rearrange("p c q j -> p q c j")
+            if on_vector:
+                nc.vector.tensor_copy(out=dst, in_=src)
+            else:
+                nc.scalar.copy(out=dst, in_=src)
+
         def quantise_tap(k):
             nc.vector.quantize_mx(
                 out=wt_codes[:, k].rearrange("p j q -> p (j q)").bitcast(FP8X4),
@@ -136,8 +145,10 @@ def tile_conditionalfeaturesupsample_kernel(
                     stop=True,
                 )
 
-        for a in range(WT_CHUNKS):
+        for a in range(WT_CHUNKS - 1):
             sort_chunk(a)
+        for k in range(KS):
+            sort_tap(WT_CHUNKS - 1, k, k == 0)
         b1_t = setup_psum.tile([P, P], BF16)
         nc.tensor.transpose(b1_t[:], b1_rows[:], ident_bf[:])
         b1_sb = keep.tile([P, N_BLOCKS], F32)
@@ -223,11 +234,10 @@ def tile_conditionalfeaturesupsample_kernel(
         def block_0_out(on_vector, h, bank_view):
             ls = slice(h * LH, (h + 1) * LH)
             add_bias_out_of_psum(nc, on_vector, y_0[:, ls], bank_view, b1_sb[:, 0:1])
-            for r in range(R):
-                nc.sync.dma_start(
-                    out=out[:, 0, 0, r * T + h * LH * KS : r * T + (h + 1) * LH * KS],
-                    in_=y_0[:, ls].rearrange("p l k -> p (l k)"),
-                )
+            nc.sync.dma_start(
+                out=out[:, 0, 0, :].rearrange("p (r t) -> p r t", r=R)[:, :, h * LH * KS : (h + 1) * LH * KS],
+                in_=y_0[:, ls].rearrange("p l k -> p (l k)").unsqueeze(1).to_broadcast([P, R, LH * KS]),
+            )
 
         up_on_scalar(0)
         for k in range(1, KS):

@@ -65,20 +65,21 @@ def tile_conditionalfeaturesupsample_kernel(
         nc.vector.memset(w1_planes[:].bitcast(I32), 0)
 
         bt_sb = keep.tile([P, PACK], BF16)
-        nc.scalar.dma_start(out=bt_sb[:], in_=bt.rearrange("(q j) -> q j", j=PACK))
-        nc.scalar.dma_start(out=b1_rows[0:N_BLOCKS, :], in_=b1.rearrange("(n p) -> n p", p=P))
         x_sb = keep.tile([P, C], BF16)
-        nc.sync.dma_start(out=x_sb[:], in_=local_features[0])
         wt_raw = keep.tile([P, PACK, C * KS], BF16)
         wt_rows = wt.rearrange("(p c) o k -> p c (o k)", c=PACK)
         chunk_cols = C * KS // WT_CHUNKS
         for a in range(WT_CHUNKS):
             cols = slice(a * chunk_cols, (a + 1) * chunk_cols)
             nc.sync.dma_start(out=wt_raw[:, :, cols], in_=wt_rows[:, :, cols])
+            if a == 0:
+                nc.sync.dma_start(out=x_sb[:], in_=local_features[0])
+        nc.sync.dma_start(out=bt_sb[:], in_=bt.rearrange("(q j) -> q j", j=PACK))
         for r in range(4):
             nc.sync.dma_start(
                 out=w1_planes[r:P:32, :].bitcast(I32), in_=w1_scales[0, r:16:4, :].bitcast(I32)
             )
+        nc.sync.dma_start(out=b1_rows[0:N_BLOCKS, :], in_=b1.rearrange("(n p) -> n p", p=P))
         w1_sb = keep.tile([P, OUT], U32, align_bytes=64)
         w1_dram = w1_words[0].rearrange("p n t -> p (n t)").bitcast(I32)
         chunk = OUT // W1_CHUNKS
@@ -89,16 +90,20 @@ def tile_conditionalfeaturesupsample_kernel(
         nc.gpsimd.tensor_copy(out=bt_f32[:], in_=bt_sb[:])
         x_words_f32 = x_sb[:].bitcast(F32)
         xt = setup_psum.tile([P, 2, L], F32)
-        for u in range(2):
-            nc.tensor.transpose(xt[:, u, :], x_words_f32[:, u : C // 2 : 2], ident_f32[:])
         x_grouped = keep.tile([P, L * PACK], BF16, align_bytes=64)
-        nc.vector.tensor_copy(
-            out=x_grouped[:].bitcast(F32).rearrange("p (l u) -> p l u", u=2),
-            in_=xt[:].rearrange("p u l -> p l u"),
-        )
         x_codes = keep.tile([P, L], U32, align_bytes=64)
         x_scales = keep.tile([P, L], U8, align_bytes=64)
-        nc.vector.quantize_mx(out=x_codes[:].bitcast(FP8X4), scales=x_scales[:], in_=x_grouped[:])
+
+        def transpose_x():
+            for u in range(2):
+                nc.tensor.transpose(xt[:, u, :], x_words_f32[:, u : C // 2 : 2], ident_f32[:])
+            nc.scalar.copy(
+                out=x_grouped[:].bitcast(F32).rearrange("p (l u) -> p l u", u=2),
+                in_=xt[:].rearrange("p u l -> p l u"),
+            )
+
+        def quantise_x():
+            nc.vector.quantize_mx(out=x_codes[:].bitcast(FP8X4), scales=x_scales[:], in_=x_grouped[:])
 
         wt_grouped = keep.tile([P, KS, PACK, P, PACK], BF16, align_bytes=64)
         wt_codes = keep.tile([P, KS, PACK, P], U32, align_bytes=64)
@@ -145,14 +150,13 @@ def tile_conditionalfeaturesupsample_kernel(
                     stop=True,
                 )
 
-        for a in range(WT_CHUNKS - 1):
-            sort_chunk(a)
+        sort_chunk(0)
+        transpose_x()
+        sort_chunk(1)
+        quantise_x()
+        sort_chunk(2)
         for k in range(KS):
             sort_tap(WT_CHUNKS - 1, k, k == 0)
-        b1_t = setup_psum.tile([P, P], BF16)
-        nc.tensor.transpose(b1_t[:], b1_rows[:], ident_bf[:])
-        b1_sb = keep.tile([P, N_BLOCKS], F32)
-        nc.scalar.copy(out=b1_sb[:], in_=b1_t[:, 0:N_BLOCKS])
         for k in range(KS):
             quantise_tap(k)
             first_product(k)
@@ -240,6 +244,10 @@ def tile_conditionalfeaturesupsample_kernel(
             )
 
         up_on_scalar(0)
+        b1_t = setup_psum.tile([P, P], BF16)
+        nc.tensor.transpose(b1_t[:], b1_rows[:], ident_bf[:])
+        b1_sb = keep.tile([P, N_BLOCKS], F32)
+        nc.scalar.copy(out=b1_sb[:], in_=b1_t[:, 0:N_BLOCKS])
         for k in range(1, KS):
             up_on_vector(0, k)
         up_on_vector(1, 1)

@@ -29,7 +29,7 @@ Y_BUFS = 4
 GROUP = 4
 FIRST_PAIRS = 1
 ACC_BANKS = 6
-VECTOR_J = 3
+VECTOR_J = (3, 2, 3)
 HALVES = 2
 LH = L // HALVES
 
@@ -115,7 +115,7 @@ def tile_conditionalfeaturesupsample_kernel(
             for j in range(PACK):
                 dst = wt_grouped[:, :, j, qs, :].rearrange("p k q c -> p q c k")
                 src = wt_raw5[:, :, qs, j, :].rearrange("p c q k -> p q c k")
-                if j < VECTOR_J:
+                if j < VECTOR_J[a]:
                     nc.vector.tensor_copy(out=dst, in_=src)
                 else:
                     nc.scalar.copy(out=dst, in_=src)
@@ -156,7 +156,9 @@ def tile_conditionalfeaturesupsample_kernel(
         quantise_x()
         sort_chunk(2)
         for k in range(KS):
-            sort_tap(WT_CHUNKS - 1, k, k == 0)
+            sort_tap(WT_CHUNKS - 1, k, k < 2)
+        b1_t = setup_psum.tile([P, P], BF16)
+        nc.tensor.transpose(b1_t[:], b1_rows[:], ident_bf[:])
         for k in range(KS):
             quantise_tap(k)
             first_product(k)
@@ -244,8 +246,6 @@ def tile_conditionalfeaturesupsample_kernel(
             )
 
         up_on_scalar(0)
-        b1_t = setup_psum.tile([P, P], BF16)
-        nc.tensor.transpose(b1_t[:], b1_rows[:], ident_bf[:])
         b1_sb = keep.tile([P, N_BLOCKS], F32)
         nc.scalar.copy(out=b1_sb[:], in_=b1_t[:, 0:N_BLOCKS])
         for k in range(1, KS):

from contextlib import ExitStack

import concourse.mybir as mybir
from concourse.masks import make_identity

F32 = mybir.dt.float32
BF16 = mybir.dt.bfloat16
I32 = mybir.dt.int32
U32 = mybir.dt.uint32
U8 = mybir.dt.uint8
FP8X4 = mybir.dt.float8_e4m3fn_x4
ADD = mybir.AluOpType.add
IDENTITY = mybir.ActivationFunctionType.Identity

P = 128
PACK = 4
L = 128
C = 512
KS = 4
T = L * KS
R = 4
OUT = 3072
N_BLOCKS = OUT // P
WT_CHUNKS = 4
Q_CHUNK = P // WT_CHUNKS
Q_HALF = 64
W1_CHUNKS = 3
Y_BUFS = 4
GROUP = 4
FIRST_PAIRS = 1
ACC_BANKS = 6
VECTOR_J = (3, 2, 3)
HALVES = 2
LH = L // HALVES

FLOPS = 2 * L * C * C * KS + 2 * OUT * C * T


def add_bias_out_of_psum(nc, on_vector, dst, src, bias):
    if on_vector:
        nc.vector.tensor_scalar(out=dst, in0=src, scalar1=bias, scalar2=None, op0=ADD)
    else:
        nc.scalar.activation(out=dst, in_=src, func=IDENTITY, bias=bias)


def tile_conditionalfeaturesupsample_kernel(
    tc, local_features, wt, bt, w1_words, w1_scales, b1, out
):
    nc = tc.nc
    with ExitStack() as ctx:
        keep = ctx.enter_context(tc.tile_pool(name="keep", bufs=1))
        y_pool = ctx.enter_context(tc.tile_pool(name="y_pool", bufs=Y_BUFS))
        setup_psum = ctx.enter_context(tc.psum_pool(name="setup_psum", bufs=1))
        acc_psum = ctx.enter_context(tc.psum_pool(name="acc_psum", bufs=ACC_BANKS))
        ctx.enter_context(tc.manual_schedule())

        b1_rows = keep.tile([P, P], BF16)
        nc.gpsimd.memset(b1_rows[:], 0.0)
        ident_f32 = keep.tile([P, P], F32)
        make_identity(nc, ident_f32[:])
        ident_bf = keep.tile([P, P], BF16)
        make_identity(nc, ident_bf[:])
        bt_f32 = keep.tile([P, PACK], F32)
        w1_planes = keep.tile([P, OUT], U8, align_bytes=64)
        nc.vector.memset(w1_planes[:].bitcast(I32), 0)

        bt_sb = keep.tile([P, PACK], BF16)
        x_sb = keep.tile([P, C], BF16)
        wt_raw = keep.tile([P, PACK, C * KS], BF16)
        wt_rows = wt.rearrange("(p c) o k -> p c (o k)", c=PACK)
        chunk_cols = C * KS // WT_CHUNKS
        for a in range(WT_CHUNKS):
            cols = slice(a * chunk_cols, (a + 1) * chunk_cols)
            nc.sync.dma_start(out=wt_raw[:, :, cols], in_=wt_rows[:, :, cols])
            if a == 0:
                nc.sync.dma_start(out=x_sb[:], in_=local_features[0])
        nc.sync.dma_start(out=bt_sb[:], in_=bt.rearrange("(q j) -> q j", j=PACK))
        for r in range(4):
            nc.sync.dma_start(
                out=w1_planes[r:P:32, :].bitcast(I32), in_=w1_scales[0, r:16:4, :].bitcast(I32)
            )
        nc.sync.dma_start(out=b1_rows[0:N_BLOCKS, :], in_=b1.rearrange("(n p) -> n p", p=P))
        w1_sb = keep.tile([P, OUT], U32, align_bytes=64)
        w1_dram = w1_words[0].rearrange("p n t -> p (n t)").bitcast(I32)
        chunk = OUT // W1_CHUNKS
        for i in range(W1_CHUNKS):
            cols = slice(i * chunk, (i + 1) * chunk)
            nc.sync.dma_start(out=w1_sb[:, cols].bitcast(I32), in_=w1_dram[:, cols])

        nc.gpsimd.tensor_copy(out=bt_f32[:], in_=bt_sb[:])
        x_words_f32 = x_sb[:].bitcast(F32)
        xt = setup_psum.tile([P, 2, L], F32)
        x_grouped = keep.tile([P, L * PACK], BF16, align_bytes=64)
        x_codes = keep.tile([P, L], U32, align_bytes=64)
        x_scales = keep.tile([P, L], U8, align_bytes=64)

        def transpose_x():
            for u in range(2):
                nc.tensor.transpose(xt[:, u, :], x_words_f32[:, u : C // 2 : 2], ident_f32[:])
            nc.scalar.copy(
                out=x_grouped[:].bitcast(F32).rearrange("p (l u) -> p l u", u=2),
                in_=xt[:].rearrange("p u l -> p l u"),
            )

        def quantise_x():
            nc.vector.quantize_mx(out=x_codes[:].bitcast(FP8X4), scales=x_scales[:], in_=x_grouped[:])

        wt_grouped = keep.tile([P, KS, PACK, P, PACK], BF16, align_bytes=64)
        wt_codes = keep.tile([P, KS, PACK, P], U32, align_bytes=64)
        wt_scales = keep.tile([P, KS, PACK, P], U8, align_bytes=64)
        wt_raw5 = wt_raw[:].rearrange("p c (q j k) -> p c q j k", j=PACK, k=KS)

        def sort_chunk(a):
            qs = slice(a * Q_CHUNK, (a + 1) * Q_CHUNK)
            for j in range(PACK):
                dst = wt_grouped[:, :, j, qs, :].rearrange("p k q c -> p q c k")
                src = wt_raw5[:, :, qs, j, :].rearrange("p c q k -> p q c k")
                if j < VECTOR_J[a]:
                    nc.vector.tensor_copy(out=dst, in_=src)
                else:
                    nc.scalar.copy(out=dst, in_=src)

        def sort_tap(a, k, on_vector):
            qs = slice(a * Q_CHUNK, (a + 1) * Q_CHUNK)
            dst = wt_grouped[:, k, :, qs, :].rearrange("p j q c -> p q c j")
            src = wt_raw5[:, :, qs, :, k].rearrange("p c q j -> p q c j")
            if on_vector:
                nc.vector.tensor_copy(out=dst, in_=src)
            else:
                nc.scalar.copy(out=dst, in_=src)

        def quantise_tap(k):
            nc.vector.quantize_mx(
                out=wt_codes[:, k].rearrange("p j q -> p (j q)").bitcast(FP8X4),
                scales=wt_scales[:, k].rearrange("p j q -> p (j q)"),
                in_=wt_grouped[:, k].rearrange("p j q c -> p (j q c)"),
            )

        up_acc = [acc_psum.tile([P, PACK, L], F32, tag="acc", name="up_acc_%d" % k) for k in range(KS)]

        def first_product(k):
            for j in range(PACK):
                nc.tensor.matmul_mx(
                    out=up_acc[k][:, j, :],
                    lhsT=wt_codes[:, k, j, :].bitcast(FP8X4),
                    lhsT_scale=wt_scales[:, k, j, :],
                    rhs=x_codes[:].bitcast(FP8X4),
                    rhs_scale=x_scales[:],
                    start=True,
                    stop=True,
                )

        sort_chunk(0)
        transpose_x()
        sort_chunk(1)
        quantise_x()
        sort_chunk(2)
        for k in range(KS):
            sort_tap(WT_CHUNKS - 1, k, k < 2)
        b1_t = setup_psum.tile([P, P], BF16)
        nc.tensor.transpose(b1_t[:], b1_rows[:], ident_bf[:])
        for k in range(KS):
            quantise_tap(k)
            first_product(k)

        up_grouped = keep.tile([P, HALVES, KS, LH, PACK], BF16, align_bytes=64)
        up_codes = keep.tile([P, HALVES, KS, LH], U32, align_bytes=64)
        up_scales = keep.tile([P, HALVES, KS, LH], U8, align_bytes=64)

        def quantise_up(h):
            nc.vector.quantize_mx(
                out=up_codes[:, h].rearrange("q k l -> q (k l)").bitcast(FP8X4),
                scales=up_scales[:, h].rearrange("q k l -> q (k l)"),
                in_=up_grouped[:, h].rearrange("q k l j -> q (k l j)"),
            )

        def up_on_scalar(h):
            for j in range(PACK):
                nc.scalar.activation(
                    out=up_grouped[:, h, 0, :, j],
                    in_=up_acc[0][:, j, h * LH : (h + 1) * LH],
                    func=IDENTITY,
                    bias=bt_f32[:, j : j + 1],
                )

        def up_on_vector(h, k):
            nc.vector.tensor_tensor(
                out=up_grouped[:, h, k],
                in0=up_acc[k][:, :, h * LH : (h + 1) * LH].rearrange("q j l -> q l j"),
                in1=bt_f32[:].unsqueeze(1).to_broadcast([P, LH, PACK]),
                op=ADD,
            )

        def second_product_half(n, h):
            n_cols = slice(n * P, (n + 1) * P)
            y_acc = acc_psum.tile([P, KS, LH], F32, tag="acc", name="y_half_%d_%d" % (n, h))
            nc.tensor.matmul_mx(
                out=y_acc[:].rearrange("p k l -> p (k l)"),
                lhsT=w1_sb[:, n_cols].bitcast(FP8X4),
                lhsT_scale=w1_planes[:, n_cols],
                rhs=up_codes[:, h].rearrange("q k l -> q (k l)").bitcast(FP8X4),
                rhs_scale=up_scales[:, h].rearrange("q k l -> q (k l)"),
                start=True,
                stop=True,
            )
            return y_acc[:].rearrange("p k l -> p l k")

        def second_product(n):
            n_cols = slice(n * P, (n + 1) * P)
            y_acc = acc_psum.tile([P, HALVES, KS, LH], F32, tag="acc")
            nc.tensor.matmul_mx(
                out=y_acc[:].rearrange("p h k l -> p (h k l)"),
                lhsT=w1_sb[:, n_cols].bitcast(FP8X4),
                lhsT_scale=w1_planes[:, n_cols],
                rhs=up_codes[:].rearrange("q h k l -> q (h k l)").bitcast(FP8X4),
                rhs_scale=up_scales[:].rearrange("q h k l -> q (h k l)"),
                start=True,
                stop=True,
            )
            return [y_acc[:, h].rearrange("p k l -> p l k") for h in range(HALVES)]

        def repeat_out_of_psum(on_vector, dst, bank_view, h, n):
            add_bias_out_of_psum(
                nc,
                on_vector,
                dst[:, :, h * LH : (h + 1) * LH],
                bank_view.unsqueeze(1).to_broadcast([P, R, LH, KS]),
                b1_sb[:, n : n + 1],
            )

        def block_out(on_vector, dst, n):
            banks = second_product(n)
            for h in range(HALVES):
                repeat_out_of_psum(on_vector, dst, banks[h], h, n)

        y_0 = keep.tile([P, L, KS], F32)
        y_1 = keep.tile([P, R, L, KS], F32)
        y_23 = keep.tile([P, 2, R, L, KS], F32)

        def block_0_out(on_vector, h, bank_view):
            ls = slice(h * LH, (h + 1) * LH)
            add_bias_out_of_psum(nc, on_vector, y_0[:, ls], bank_view, b1_sb[:, 0:1])
            nc.sync.dma_start(
                out=out[:, 0, 0, :].rearrange("p (r t) -> p r t", r=R)[:, :, h * LH * KS : (h + 1) * LH * KS],
                in_=y_0[:, ls].rearrange("p l k -> p (l k)").unsqueeze(1).to_broadcast([P, R, LH * KS]),
            )

        up_on_scalar(0)
        b1_sb = keep.tile([P, N_BLOCKS], F32)
        nc.scalar.copy(out=b1_sb[:], in_=b1_t[:, 0:N_BLOCKS])
        for k in range(1, KS):
            up_on_vector(0, k)
        up_on_vector(1, 1)
        quantise_up(0)
        up_on_scalar(1)
        banks_0 = [second_product_half(n, 0) for n in range(2)]
        up_on_vector(1, 2)
        up_on_vector(1, 3)
        block_0_out(False, 0, banks_0[0])
        repeat_out_of_psum(False, y_1, banks_0[1], 0, 1)
        quantise_up(1)
        banks_1 = [second_product_half(n, 1) for n in range(2)]
        block_0_out(True, 1, banks_1[0])
        repeat_out_of_psum(True, y_1, banks_1[1], 1, 1)
        nc.sync.dma_start(out=out[:, 0, 1, :], in_=y_1[:].rearrange("p r l k -> p (r l k)"))
        block_out(False, y_23[:, 0], 2)
        block_out(True, y_23[:, 1], 3)
        nc.sync.dma_start(out=out[:, 0, 2:4, :], in_=y_23[:].rearrange("p e r l k -> p e (r l k)"))

        for n0 in range(GROUP, N_BLOCKS, GROUP):
            y_sb = y_pool.tile([P, GROUP, R, L, KS], F32)
            for e in range(GROUP):
                block_out(e % 2 == 1, y_sb[:, e], n0 + e)
            nc.sync.dma_start(
                out=out[:, 0, n0 : n0 + GROUP, :],
                in_=y_sb[:].rearrange("p e r l k -> p e (r l k)"),
            )
